import numpy as np
import ml_dtypes


def mxq(x, axis, fmt="e4m3"):
    dtype, down = {"e4m3": (ml_dtypes.float8_e4m3fn, 7), "e5m2": (ml_dtypes.float8_e5m2, 14)}[fmt]
    v = np.moveaxis(np.asarray(x, np.float32).astype(ml_dtypes.bfloat16).astype(np.float64), axis, -1)
    blocks = v.reshape(v.shape[:-1] + (-1, 32))
    amax = np.abs(blocks).max(-1, keepdims=True)
    byte = np.maximum(np.where(amax > 0, np.frexp(amax)[1] - 1 + 127, 0) - down, 1)
    scale = np.exp2(byte - 127.0)
    codes = (blocks / scale).astype(np.float32).astype(dtype).astype(np.float64)
    return np.moveaxis((codes * scale).reshape(v.shape), -1, axis)


WIDE = False


def mx_kscale(k):
    if not WIDE:
        return np.ones(k)
    levels = np.array([10, -10, 5, -5, 0])
    if k % 512:
        return np.exp2(np.random.permutation(np.resize(levels, k // 32))).repeat(32)
    a = np.empty((k // 512, 16))
    for p in range(k // 512):
        a[p, :8] = np.random.permutation(np.resize(levels, 8))
        for g in range(8):
            far = levels[np.abs(levels - a[p, g]) >= 10]
            a[p, g + 8] = far[np.random.randint(len(far))]
    return np.exp2(a.ravel()).repeat(32)


BF16 = ml_dtypes.bfloat16


def bf(x):
    return np.asarray(x, np.float32).astype(BF16)


def f64(x):
    return np.asarray(x).astype(np.float64)


B, DIM, D2, T = 1, 512, 1024, 512


def setup_inputs():
    s = mx_kscale(D2)
    es = 0.25 * s[None, :, None]
    ws = 0.35 / np.sqrt(D2) / s[:, None] / s[None, :]
    return {"E_re": bf(np.random.standard_normal((B, D2, T)) * es),
            "E_im": bf(np.random.standard_normal((B, D2, T)) * es),
            "WKQ_re": bf(np.random.standard_normal((D2, D2)) * ws),
            "WKQ_im": bf(np.random.standard_normal((D2, D2)) * ws)}


def reference(E_re, E_im, WKQ_re, WKQ_im):
    er = mxq(f64(E_re), 1, "e4m3")
    ei = mxq(f64(E_im), 1, "e4m3")
    wr = mxq(f64(WKQ_re), 1, "e4m3")
    wi = mxq(f64(WKQ_im), 1, "e4m3")
    q_re = (wr @ er) - (wi @ ei)
    q_im = (wr @ ei) + (wi @ er)
    qr = mxq(q_re, 1, "e4m3")
    qi = mxq(q_im, 1, "e4m3")
    ert = er.transpose(0, 2, 1)
    eit = ei.transpose(0, 2, 1)
    s_re = (ert @ qr) + (eit @ qi)
    s_im = (ert @ qi) - (eit @ qr)
    return s_re, s_im

@@ -1,0 +1,218 @@
+from contextlib import ExitStack
+
+import concourse.mybir as mybir
+from concourse.masks import make_identity
+
+BF16 = mybir.dt.bfloat16
+F32 = mybir.dt.float32
+U32 = mybir.dt.uint32
+U8 = mybir.dt.uint8
+FP8X4 = mybir.dt.float8_e4m3fn_x4
+
+P = 128
+PACK = 4
+CHANNELS = 1024
+POSITIONS = 512
+PASSES = CHANNELS // (P * PACK)
+BANK = 512
+PAIRS = CHANNELS // (2 * P)
+POSITION_TILES = POSITIONS // P
+VECTOR_POSITIONS = 352
+
+FLOPS = 2 * 4 * CHANNELS * CHANNELS * POSITIONS + 2 * 4 * POSITIONS * CHANNELS * POSITIONS
+
+STAGE1_E = {"re": ("re", "neg"), "im": ("im", "re")}
+STAGE2_TERMS = {"re": (("re", "re"), ("im", "im")), "im": (("re", "im"), ("neg", "re"))}
+
+
+def regroup(engine_copy, grouped, rows, first, last):
+    engine_copy(
+        out=grouped.rearrange("p (c i j) -> p c j i", i=4, j=PACK)[:, first // 4 : last // 4, :, :],
+        in_=rows.rearrange("p j (c i) -> p c j i", i=4)[:, first // 4 : last // 4, :, :],
+    )
+
+
+def tile_autoregressivelsa_pa_kernel(tc, E_re, E_im, WKQ_re, WKQ_im, out_0, out_1):
+    nc = tc.nc
+    e_dram = {"re": E_re, "im": E_im}
+    w_dram = {"re": WKQ_re, "im": WKQ_im}
+    s_dram = {"re": out_0, "im": out_1}
+
+    with ExitStack() as ctx:
+        keep = ctx.enter_context(tc.tile_pool(name="keep", bufs=1))
+        left_banks = ctx.enter_context(tc.psum_pool(name="left_banks", bufs=4))
+        right_banks = ctx.enter_context(tc.psum_pool(name="right_banks", bufs=4))
+        ctx.enter_context(tc.manual_schedule())
+
+        identity = keep.tile([P, P], F32, name="identity")
+        make_identity(nc, identity[:])
+
+        e_raw = {}
+        for x in ("re", "im"):
+            e_raw[x] = keep.tile([P, PASSES, PACK, POSITIONS], BF16, name="e_raw_" + x)
+        e_codes = {}
+        e_scales = {}
+        for x in ("re", "im", "neg"):
+            e_codes[x] = keep.tile([P, PASSES, POSITIONS], U32, name="e_codes_" + x, align_bytes=64)
+            e_scales[x] = keep.tile([P, PASSES, POSITIONS], U8, name="e_scales_" + x, align_bytes=64)
+        w_raw = {}
+        for q in range(PAIRS):
+            for x in ("re", "im"):
+                w_raw[(x, q)] = keep.tile([P, 2, CHANNELS], BF16, name="w_raw_%s%d" % (x, q))
+        w_codes = keep.tile([P, PAIRS, 2, 2 * PASSES * P], U32, name="w_codes", align_bytes=64)
+        w_scales = keep.tile([P, PAIRS, 2, 2 * PASSES * P], U8, name="w_scales", align_bytes=64)
+        q_raw = {}
+        q_codes = {}
+        q_scales = {}
+        for part in ("re", "im"):
+            q_raw[part] = keep.tile([P, PAIRS, 2, POSITIONS], BF16, name="q_raw_" + part)
+            q_codes[part] = keep.tile([P, PASSES, POSITIONS], U32, name="q_codes_" + part, align_bytes=64)
+            q_scales[part] = keep.tile([P, PASSES, POSITIONS], U8, name="q_scales_" + part, align_bytes=64)
+
+        def load_e(g):
+            for x in ("re", "im"):
+                nc.sync.dma_start(
+                    out=e_raw[x][:, g, :, :].rearrange("p j t -> p (j t)"),
+                    in_=e_dram[x].rearrange("b (g p j) t -> b g p (j t)", g=PASSES, p=P, j=PACK)[0, g, :, :],
+                )
+
+        def load_w(q):
+            for e in range(2):
+                for x in ("re", "im"):
+                    nc.sync.dma_start(
+                        out=w_raw[(x, q)][:, e, :],
+                        in_=w_dram[x].rearrange("(g p j) c -> g j p c", g=PASSES, p=P, j=PACK)[
+                            q // 2, 2 * (q % 2) + e, :, :
+                        ],
+                    )
+
+        load_e(0)
+        load_w(0)
+        load_e(1)
+        for q in range(1, PAIRS):
+            load_w(q)
+
+        e_grouped = {}
+        for g in range(PASSES):
+            for x in ("re", "im", "neg"):
+                e_grouped[(x, g)] = keep.tile(
+                    [P, PACK * POSITIONS], BF16, name="e_grp_%s%d" % (x, g), align_bytes=64
+                )
+
+        def quantise_e(x, g):
+            nc.vector.quantize_mx(
+                out=e_codes[x][:, g, :].bitcast(FP8X4), scales=e_scales[x][:, g, :], in_=e_grouped[(x, g)][:]
+            )
+
+        def prepare_e(g):
+            for x in ("re", "im"):
+                regroup(nc.vector.tensor_copy, e_grouped[(x, g)][:], e_raw[x][:, g, :, :], 0, VECTOR_POSITIONS)
+                regroup(nc.scalar.copy, e_grouped[(x, g)][:], e_raw[x][:, g, :, :], VECTOR_POSITIONS, POSITIONS)
+            quantise_e("re", g)
+            nc.vector.tensor_scalar_mul(out=e_grouped[("neg", g)][:], in0=e_grouped[("im", g)][:], scalar1=-1.0)
+            quantise_e("im", g)
+
+        def transpose_w(q):
+            grouped = []
+            for e in range(2):
+                words_out = keep.tile([P, 2 * BANK], F32, name="w_grp_%d%d" % (q, e), align_bytes=64)
+                grouped.append(words_out)
+                for xi, x in enumerate(("re", "im")):
+                    words_in = w_raw[(x, q)][:, e, :].bitcast(F32)
+                    bank = left_banks.tile([P, BANK], F32, name="w_bank", tag="left")
+                    for g in range(PASSES):
+                        for u in range(2):
+                            nc.tensor.transpose(
+                                bank[:, (2 * g + u) * P : (2 * g + u + 1) * P],
+                                words_in[:, 2 * P * g + u : 2 * P * (g + 1) : 2],
+                                identity[:],
+                            )
+                    nc.scalar.copy(
+                        out=words_out[:, xi * BANK : (xi + 1) * BANK].rearrange(
+                            "p (g m u) -> p g m u", g=PASSES, m=P, u=2
+                        ),
+                        in_=bank[:].rearrange("p (g u m) -> p g m u", g=PASSES, u=2, m=P),
+                    )
+            return grouped
+
+        def quantise_w(q, e, grouped):
+            nc.vector.quantize_mx(
+                out=w_codes[:, q, e, :].bitcast(FP8X4),
+                scales=w_scales[:, q, e, :],
+                in_=grouped[e][:].bitcast(BF16),
+            )
+
+        def stage1_passes(q, g, part, q_acc):
+            for e in range(2):
+                for xi, operand in enumerate(STAGE1_E[part]):
+                    w_cols = slice((xi * PASSES + g) * P, (xi * PASSES + g + 1) * P)
+                    nc.tensor.matmul_mx(
+                        out=q_acc[(e, part)][:],
+                        lhsT=w_codes[:, q, e, w_cols].bitcast(FP8X4),
+                        lhsT_scale=w_scales[:, q, e, w_cols],
+                        rhs=e_codes[operand][:, g, :].bitcast(FP8X4),
+                        rhs_scale=e_scales[operand][:, g, :],
+                        start=(g == 0 and xi == 0),
+                        stop=(g == PASSES - 1 and xi == 1),
+                    )
+                if g == PASSES - 1:
+                    nc.scalar.copy(out=q_raw[part][:, q, e, :], in_=q_acc[(e, part)][:])
+
+        def quantise_q(g):
+            for part in ("im", "re"):
+                grouped = keep.tile([P, PACK * POSITIONS], BF16, name="q_grp_%s%d" % (part, g), align_bytes=64)
+                rows = q_raw[part][:, 2 * g : 2 * g + 2, :, :].rearrange("p u e t -> p (u e) t")
+                regroup(nc.vector.tensor_copy, grouped[:], rows, 0, POSITIONS)
+                nc.vector.quantize_mx(
+                    out=q_codes[part][:, g, :].bitcast(FP8X4), scales=q_scales[part][:, g, :], in_=grouped[:]
+                )
+
+        prepare_e(0)
+        w_grouped = transpose_w(0)
+        quantise_w(0, 0, w_grouped)
+        quantise_e("neg", 0)
+        quantise_w(0, 1, w_grouped)
+        prepare_e(1)
+        quantise_e("neg", 1)
+        for q in range(PAIRS):
+            q_acc = {}
+            for part in ("im", "re"):
+                for e in range(2):
+                    q_acc[(e, part)] = right_banks.tile([P, BANK], F32, name="q_acc", tag="right")
+            stage1_passes(q, 0, "im", q_acc)
+            if q + 1 < PAIRS:
+                w_grouped = transpose_w(q + 1)
+                quantise_w(q + 1, 0, w_grouped)
+                quantise_w(q + 1, 1, w_grouped)
+            stage1_passes(q, 0, "re", q_acc)
+            stage1_passes(q, 1, "im", q_acc)
+            stage1_passes(q, 1, "re", q_acc)
+            if q % 2 == 1:
+                quantise_q(q // 2)
+
+        s_banks = {"re": (left_banks, "left"), "im": (right_banks, "right")}
+        s_acc = {}
+        for g in range(PASSES):
+            for part in ("re", "im"):
+                for i in range(POSITION_TILES):
+                    if g == 0:
+                        pool, tag = s_banks[part]
+                        s_acc[(part, i)] = pool.tile([P, BANK], F32, name="s_acc", tag=tag)
+                    rows = slice(i * P, (i + 1) * P)
+                    for n, (operand, q_part) in enumerate(STAGE2_TERMS[part]):
+                        nc.tensor.matmul_mx(
+                            out=s_acc[(part, i)][:],
+                            lhsT=e_codes[operand][:, g, rows].bitcast(FP8X4),
+                            lhsT_scale=e_scales[operand][:, g, rows],
+                            rhs=q_codes[q_part][:, g, :].bitcast(FP8X4),
+                            rhs_scale=q_scales[q_part][:, g, :],
+                            start=(g == 0 and n == 0),
+                            stop=(g == PASSES - 1 and n == 1),
+                        )
+                    if g == PASSES - 1:
+                        s_sb = keep.tile([P, POSITIONS], F32, name="s_sb_%s%d" % (part, i))
+                        if i % 2 == 0:
+                            nc.scalar.copy(out=s_sb[:], in_=s_acc[(part, i)][:])
+                        else:
+                            nc.vector.tensor_copy(out=s_sb[:], in_=s_acc[(part, i)][:])
+                        nc.sync.dma_start(out=s_dram[part][0, rows, :], in_=s_sb[:])

@@ -112,6 +112,18 @@ def tile_autoregressivelsa_pa_kernel(tc, E_re, E_im, WKQ_re, WKQ_im, out_0, out_
             nc.vector.tensor_scalar_mul(out=e_grouped[("neg", g)][:], in0=e_grouped[("im", g)][:], scalar1=-1.0)
             quantise_e("im", g)
 
+        w_perm = {}
+
+        def permute_w(q):
+            for x in ("re", "im"):
+                w_perm[(x, q)] = keep.tile([P, 2 * PASSES, 2, P], F32, name="w_perm_%s%d" % (x, q))
+                nc.vector.tensor_copy(
+                    out=w_perm[(x, q)][:],
+                    in_=w_raw[(x, q)][:].rearrange("p e c -> p (e c)").bitcast(F32).rearrange(
+                        "p (g c u) -> p g u c", g=2 * PASSES, c=P, u=2
+                    ),
+                )
+
         def transpose_w(q):
             grouped = []
             for e in range(2):
@@ -122,11 +134,11 @@ def tile_autoregressivelsa_pa_kernel(tc, E_re, E_im, WKQ_re, WKQ_im, out_0, out_
                     bank = left_banks.tile([P, BANK], F32, name="w_bank", tag="left")
                     for g in range(PASSES):
                         for u in range(2):
-                            nc.tensor.transpose(
-                                bank[:, (2 * g + u) * P : (2 * g + u + 1) * P],
-                                words_in[:, 2 * P * g + u : 2 * P * (g + 1) : 2],
-                                identity[:],
-                            )
+                            if (x, q) in w_perm:
+                                in_ = w_perm[(x, q)][:, PASSES * e + g, u, :]
+                            else:
+                                in_ = words_in[:, 2 * P * g + u : 2 * P * (g + 1) : 2]
+                            nc.tensor.transpose(bank[:, (2 * g + u) * P : (2 * g + u + 1) * P], in_, identity[:])
                     nc.scalar.copy(
                         out=words_out[:, xi * BANK : (xi + 1) * BANK].rearrange(
                             "p (g m u) -> p g m u", g=PASSES, m=P, u=2
@@ -184,6 +196,8 @@ def tile_autoregressivelsa_pa_kernel(tc, E_re, E_im, WKQ_re, WKQ_im, out_0, out_
                 w_grouped = transpose_w(q + 1)
                 quantise_w(q + 1, 0, w_grouped)
                 quantise_w(q + 1, 1, w_grouped)
+            if q + 2 < PAIRS:
+                permute_w(q + 2)
             stage1_passes(q, 0, "re", q_acc)
             stage1_passes(q, 1, "im", q_acc)
             stage1_passes(q, 1, "re", q_acc)

@@ -15,9 +15,11 @@ CHANNELS = 1024
 POSITIONS = 512
 PASSES = CHANNELS // (P * PACK)
 BANK = 512
-PAIRS = CHANNELS // (2 * P)
+TILES = CHANNELS // P
 POSITION_TILES = POSITIONS // P
-VECTOR_POSITIONS = 352
+HEAD_TILES = 3
+BLOCK_TILES = (6, 7)
+VECTOR_POSITIONS = {("im", 0): 352, ("im", 1): 352, ("re", 0): 352, ("re", 1): 352}
 
 FLOPS = 2 * 4 * CHANNELS * CHANNELS * POSITIONS + 2 * 4 * POSITIONS * CHANNELS * POSITIONS
 
@@ -48,161 +50,248 @@ def tile_autoregressivelsa_pa_kernel(tc, E_re, E_im, WKQ_re, WKQ_im, out_0, out_
         make_identity(nc, identity[:])
 
         e_raw = {}
-        for x in ("re", "im"):
-            e_raw[x] = keep.tile([P, PASSES, PACK, POSITIONS], BF16, name="e_raw_" + x)
+        e_grouped = {}
+        for x in ("re", "im", "neg"):
+            for g in range(PASSES):
+                if x != "neg":
+                    e_raw[(x, g)] = keep.tile([P, PACK, POSITIONS], BF16, name="e_raw_%s%d" % (x, g))
+                e_grouped[(x, g)] = keep.tile(
+                    [P, PACK * POSITIONS], BF16, name="e_grp_%s%d" % (x, g), align_bytes=64
+                )
         e_codes = {}
         e_scales = {}
         for x in ("re", "im", "neg"):
             e_codes[x] = keep.tile([P, PASSES, POSITIONS], U32, name="e_codes_" + x, align_bytes=64)
             e_scales[x] = keep.tile([P, PASSES, POSITIONS], U8, name="e_scales_" + x, align_bytes=64)
         w_raw = {}
-        for q in range(PAIRS):
-            for x in ("re", "im"):
-                w_raw[(x, q)] = keep.tile([P, 2, CHANNELS], BF16, name="w_raw_%s%d" % (x, q))
-        w_codes = keep.tile([P, PAIRS, 2, 2 * PASSES * P], U32, name="w_codes", align_bytes=64)
-        w_scales = keep.tile([P, PAIRS, 2, 2 * PASSES * P], U8, name="w_scales", align_bytes=64)
+        for m in range(TILES):
+            if m in BLOCK_TILES:
+                w_raw[m] = keep.tile([P, 2, PASSES, 4, P], BF16, name="w_raw%d" % m)
+            else:
+                w_raw[m] = keep.tile([P, 2, CHANNELS], BF16, name="w_raw%d" % m)
+        w_codes = keep.tile([P, TILES, 2 * PASSES * P], U32, name="w_codes", align_bytes=64)
+        w_scales = keep.tile([P, TILES, 2 * PASSES * P], U8, name="w_scales", align_bytes=64)
         q_raw = {}
         q_codes = {}
         q_scales = {}
         for part in ("re", "im"):
-            q_raw[part] = keep.tile([P, PAIRS, 2, POSITIONS], BF16, name="q_raw_" + part)
+            q_raw[part] = keep.tile([P, TILES, POSITIONS], BF16, name="q_raw_" + part)
             q_codes[part] = keep.tile([P, PASSES, POSITIONS], U32, name="q_codes_" + part, align_bytes=64)
             q_scales[part] = keep.tile([P, PASSES, POSITIONS], U8, name="q_scales_" + part, align_bytes=64)
 
-        def load_e(g):
-            for x in ("re", "im"):
+        def load_e(x, g):
+            nc.sync.dma_start(
+                out=e_raw[(x, g)][:].rearrange("p j t -> p (j t)"),
+                in_=e_dram[x].rearrange("b (g p j) t -> b g p (j t)", g=PASSES, p=P, j=PACK)[0, g, :, :],
+            )
+
+        def load_w_blocks(m):
+            for xi, x in enumerate(("re", "im")):
+                for g in range(PASSES):
+                    for a in range(4):
+                        nc.sync.dma_start(
+                            out=w_raw[m][32 * a : 32 * a + 32, xi, g, :, :],
+                            in_=w_dram[x].rearrange("(h n r t) (g a k) -> h t g a r n k", n=4, r=32, t=PACK, g=PASSES, a=4)[
+                                m // 4, m % 4, g, a, :, :, :
+                            ],
+                        )
+
+        def load_w(m):
+            for xi, x in enumerate(("re", "im")):
                 nc.sync.dma_start(
-                    out=e_raw[x][:, g, :, :].rearrange("p j t -> p (j t)"),
-                    in_=e_dram[x].rearrange("b (g p j) t -> b g p (j t)", g=PASSES, p=P, j=PACK)[0, g, :, :],
+                    out=w_raw[m][:, xi, :],
+                    in_=w_dram[x].rearrange("(g p j) c -> g j p c", g=PASSES, p=P, j=PACK)[m // 4, m % 4, :, :],
                 )
 
-        def load_w(q):
-            for e in range(2):
-                for x in ("re", "im"):
-                    nc.sync.dma_start(
-                        out=w_raw[(x, q)][:, e, :],
-                        in_=w_dram[x].rearrange("(g p j) c -> g j p c", g=PASSES, p=P, j=PACK)[
-                            q // 2, 2 * (q % 2) + e, :, :
-                        ],
-                    )
-
-        load_e(0)
+        load_e("im", 0)
         load_w(0)
-        load_e(1)
-        for q in range(1, PAIRS):
-            load_w(q)
+        load_w(1)
+        load_e("im", 1)
+        load_w(2)
+        load_e("re", 0)
+        load_w(3)
+        load_e("re", 1)
+        load_w(4)
+        load_w(5)
+        for m in BLOCK_TILES:
+            load_w_blocks(m)
 
-        e_grouped = {}
-        for g in range(PASSES):
-            for x in ("re", "im", "neg"):
-                e_grouped[(x, g)] = keep.tile(
-                    [P, PACK * POSITIONS], BF16, name="e_grp_%s%d" % (x, g), align_bytes=64
-                )
+        def regroup_e(x, g):
+            cut = VECTOR_POSITIONS[(x, g)]
+            regroup(nc.vector.tensor_copy, e_grouped[(x, g)][:], e_raw[(x, g)][:], 0, cut)
+            regroup(nc.scalar.copy, e_grouped[(x, g)][:], e_raw[(x, g)][:], cut, POSITIONS)
+
+        def negate_e(g):
+            nc.vector.tensor_scalar_mul(out=e_grouped[("neg", g)][:], in0=e_grouped[("im", g)][:], scalar1=-1.0)
 
         def quantise_e(x, g):
             nc.vector.quantize_mx(
                 out=e_codes[x][:, g, :].bitcast(FP8X4), scales=e_scales[x][:, g, :], in_=e_grouped[(x, g)][:]
             )
 
-        def prepare_e(g):
-            for x in ("re", "im"):
-                regroup(nc.vector.tensor_copy, e_grouped[(x, g)][:], e_raw[x][:, g, :, :], 0, VECTOR_POSITIONS)
-                regroup(nc.scalar.copy, e_grouped[(x, g)][:], e_raw[x][:, g, :, :], VECTOR_POSITIONS, POSITIONS)
-            quantise_e("re", g)
-            nc.vector.tensor_scalar_mul(out=e_grouped[("neg", g)][:], in0=e_grouped[("im", g)][:], scalar1=-1.0)
-            quantise_e("im", g)
-
+        w_grouped = {}
         w_perm = {}
+        w_turned = {}
 
-        def permute_w(q):
-            for x in ("re", "im"):
-                w_perm[(x, q)] = keep.tile([P, 2 * PASSES, 2, P], F32, name="w_perm_%s%d" % (x, q))
-                nc.vector.tensor_copy(
-                    out=w_perm[(x, q)][:],
-                    in_=w_raw[(x, q)][:].rearrange("p e c -> p (e c)").bitcast(F32).rearrange(
-                        "p (g c u) -> p g u c", g=2 * PASSES, c=P, u=2
-                    ),
-                )
-
-        def transpose_w(q):
-            grouped = []
-            for e in range(2):
-                words_out = keep.tile([P, 2 * BANK], F32, name="w_grp_%d%d" % (q, e), align_bytes=64)
-                grouped.append(words_out)
-                for xi, x in enumerate(("re", "im")):
-                    words_in = w_raw[(x, q)][:, e, :].bitcast(F32)
-                    bank = left_banks.tile([P, BANK], F32, name="w_bank", tag="left")
-                    for g in range(PASSES):
-                        for u in range(2):
-                            if (x, q) in w_perm:
-                                in_ = w_perm[(x, q)][:, PASSES * e + g, u, :]
-                            else:
-                                in_ = words_in[:, 2 * P * g + u : 2 * P * (g + 1) : 2]
-                            nc.tensor.transpose(bank[:, (2 * g + u) * P : (2 * g + u + 1) * P], in_, identity[:])
-                    nc.scalar.copy(
-                        out=words_out[:, xi * BANK : (xi + 1) * BANK].rearrange(
-                            "p (g m u) -> p g m u", g=PASSES, m=P, u=2
-                        ),
-                        in_=bank[:].rearrange("p (g u m) -> p g m u", g=PASSES, u=2, m=P),
-                    )
-            return grouped
-
-        def quantise_w(q, e, grouped):
-            nc.vector.quantize_mx(
-                out=w_codes[:, q, e, :].bitcast(FP8X4),
-                scales=w_scales[:, q, e, :],
-                in_=grouped[e][:].bitcast(BF16),
+        def permute_w(m):
+            w_perm[m] = keep.tile([P, 2 * PASSES, 2, P], F32, name="w_perm%d" % m)
+            nc.vector.tensor_copy(
+                out=w_perm[m][:],
+                in_=w_raw[m][:].rearrange("p x c -> p (x c)").bitcast(F32).rearrange(
+                    "p (g c u) -> p g u c", g=2 * PASSES, c=P, u=2
+                ),
             )
 
-        def stage1_passes(q, g, part, q_acc):
-            for e in range(2):
-                for xi, operand in enumerate(STAGE1_E[part]):
-                    w_cols = slice((xi * PASSES + g) * P, (xi * PASSES + g + 1) * P)
-                    nc.tensor.matmul_mx(
-                        out=q_acc[(e, part)][:],
-                        lhsT=w_codes[:, q, e, w_cols].bitcast(FP8X4),
-                        lhsT_scale=w_scales[:, q, e, w_cols],
-                        rhs=e_codes[operand][:, g, :].bitcast(FP8X4),
-                        rhs_scale=e_scales[operand][:, g, :],
-                        start=(g == 0 and xi == 0),
-                        stop=(g == PASSES - 1 and xi == 1),
-                    )
-                if g == PASSES - 1:
-                    nc.scalar.copy(out=q_raw[part][:, q, e, :], in_=q_acc[(e, part)][:])
-
-        def quantise_q(g):
-            for part in ("im", "re"):
-                grouped = keep.tile([P, PACK * POSITIONS], BF16, name="q_grp_%s%d" % (part, g), align_bytes=64)
-                rows = q_raw[part][:, 2 * g : 2 * g + 2, :, :].rearrange("p u e t -> p (u e) t")
-                regroup(nc.vector.tensor_copy, grouped[:], rows, 0, POSITIONS)
-                nc.vector.quantize_mx(
-                    out=q_codes[part][:, g, :].bitcast(FP8X4), scales=q_scales[part][:, g, :], in_=grouped[:]
+        def transpose_w(m):
+            w_grouped[m] = keep.tile([P, 2 * BANK], F32, name="w_grp_%d" % m, align_bytes=64)
+            for xi in range(2):
+                words_in = w_raw[m][:, xi, :].bitcast(F32)
+                bank = left_banks.tile([P, BANK], F32, name="w_bank", tag="left")
+                for g in range(PASSES):
+                    for u in range(2):
+                        if m in w_perm:
+                            in_ = w_perm[m][:, PASSES * xi + g, u, :]
+                        else:
+                            in_ = words_in[:, 2 * P * g + u : 2 * P * (g + 1) : 2]
+                        nc.tensor.transpose(bank[:, (2 * g + u) * P : (2 * g + u + 1) * P], in_, identity[:])
+                nc.scalar.copy(
+                    out=w_grouped[m][:, xi * BANK : (xi + 1) * BANK].rearrange(
+                        "p (g m u) -> p g m u", g=PASSES, m=P, u=2
+                    ),
+                    in_=bank[:].rearrange("p (g u m) -> p g m u", g=PASSES, u=2, m=P),
                 )
 
-        prepare_e(0)
-        w_grouped = transpose_w(0)
-        quantise_w(0, 0, w_grouped)
-        quantise_e("neg", 0)
-        quantise_w(0, 1, w_grouped)
-        prepare_e(1)
-        quantise_e("neg", 1)
-        for q in range(PAIRS):
-            q_acc = {}
+        def spread_words(m):
+            w_perm[m] = keep.tile([P, 2 * BANK], F32, name="w_perm%d" % m, align_bytes=64)
+            nc.vector.tensor_copy(
+                out=w_perm[m][:].rearrange("p (s u c) -> p s u c", u=2, c=32),
+                in_=w_raw[m][:].rearrange("p x g n k -> p (x g n k)").bitcast(F32).rearrange(
+                    "p (s c u) -> p s u c", c=32, u=2
+                ),
+            )
+
+        def turn_blocks(m):
+            w_turned[m] = keep.tile([P, 2 * BANK], F32, name="w_turned%d" % m, align_bytes=64)
+            nc.vector.transpose(out=w_turned[m][:], in_=w_perm[m][:])
+
+        def join_words(m):
+            w_grouped[m] = keep.tile([P, 2 * BANK], F32, name="w_grp_%d" % m, align_bytes=64)
+            nc.scalar.copy(
+                out=w_grouped[m][:].rearrange("p (s r u) -> p s r u", r=32, u=2),
+                in_=w_turned[m][:].rearrange("p (s u r) -> p s r u", u=2, r=32),
+            )
+
+        def quantise_w(m):
+            nc.vector.quantize_mx(
+                out=w_codes[:, m, :].bitcast(FP8X4), scales=w_scales[:, m, :], in_=w_grouped[m][:].bitcast(BF16)
+            )
+
+        q_acc = {}
+        q_done = {}
+
+        def product(m, part, g, xi):
+            if (m, part) not in q_acc:
+                q_acc[(m, part)] = right_banks.tile([P, BANK], F32, name="q_acc", tag="right")
+                q_done[(m, part)] = 0
+            acc = q_acc[(m, part)]
+            operand = STAGE1_E[part][xi]
+            w_cols = slice((xi * PASSES + g) * P, (xi * PASSES + g + 1) * P)
+            nc.tensor.matmul_mx(
+                out=acc[:],
+                lhsT=w_codes[:, m, w_cols].bitcast(FP8X4),
+                lhsT_scale=w_scales[:, m, w_cols],
+                rhs=e_codes[operand][:, g, :].bitcast(FP8X4),
+                rhs_scale=e_scales[operand][:, g, :],
+                start=q_done[(m, part)] == 0,
+                stop=q_done[(m, part)] == 3,
+            )
+            q_done[(m, part)] += 1
+
+        def out_q(m, part):
+            nc.scalar.copy(out=q_raw[part][:, m, :], in_=q_acc[(m, part)][:])
+
+        def products_im(m, g):
+            product(m, "im", g, 0)
+            product(m, "re", g, 1)
+
+        def products_re(m, g):
+            product(m, "im", g, 1)
+            product(m, "re", g, 0)
+
+        def whole_tile(m):
             for part in ("im", "re"):
-                for e in range(2):
-                    q_acc[(e, part)] = right_banks.tile([P, BANK], F32, name="q_acc", tag="right")
-            stage1_passes(q, 0, "im", q_acc)
-            if q + 1 < PAIRS:
-                w_grouped = transpose_w(q + 1)
-                quantise_w(q + 1, 0, w_grouped)
-                quantise_w(q + 1, 1, w_grouped)
-            if q + 2 < PAIRS:
-                permute_w(q + 2)
-            stage1_passes(q, 0, "re", q_acc)
-            stage1_passes(q, 1, "im", q_acc)
-            stage1_passes(q, 1, "re", q_acc)
-            if q % 2 == 1:
-                quantise_q(q // 2)
+                for g in range(PASSES):
+                    for xi in range(2):
+                        product(m, part, g, xi)
+                out_q(m, part)
+
+        q_grouped = {}
+
+        def regroup_q(part, g):
+            q_grouped[(part, g)] = keep.tile([P, PACK * POSITIONS], BF16, name="q_grp_%s%d" % (part, g), align_bytes=64)
+            regroup(nc.vector.tensor_copy, q_grouped[(part, g)][:], q_raw[part][:, 4 * g : 4 * g + 4, :], 0, POSITIONS)
+
+        def quantise_q(part, g):
+            nc.vector.quantize_mx(
+                out=q_codes[part][:, g, :].bitcast(FP8X4), scales=q_scales[part][:, g, :], in_=q_grouped[(part, g)][:]
+            )
+        regroup_e("im", 0)
+        negate_e(0)
+        quantise_e("im", 0)
+        transpose_w(0)
+        transpose_w(1)
+        quantise_w(0)
+        quantise_e("neg", 0)
+        regroup_e("im", 1)
+        quantise_w(1)
+        negate_e(1)
+        quantise_e("im", 1)
+        quantise_e("neg", 1)
+        products_im(0, 0)
+        transpose_w(2)
+        products_im(1, 0)
+        regroup_e("re", 0)
+        quantise_e("re", 0)
+        transpose_w(3)
+        products_im(0, 1)
+        products_im(1, 1)
+        regroup_e("re", 1)
+        quantise_e("re", 1)
+        transpose_w(4)
+        quantise_w(2)
+        quantise_w(3)
+        products_re(0, 0)
+        products_re(0, 1)
+        out_q(0, "im")
+        out_q(0, "re")
+        products_re(1, 0)
+        products_re(1, 1)
+        transpose_w(5)
+        out_q(1, "im")
+        out_q(1, "re")
+        spread_words(6)
+        quantise_w(4)
+        turn_blocks(6)
+        quantise_w(5)
+        whole_tile(2)
+        join_words(6)
+        spread_words(7)
+        quantise_w(6)
+        turn_blocks(7)
+        whole_tile(3)
+        regroup_q("im", 0)
+        regroup_q("re", 0)
+        whole_tile(4)
+        join_words(7)
+        quantise_q("im", 0)
+        quantise_w(7)
+        quantise_q("re", 0)
+        for m in range(5, TILES):
+            whole_tile(m)
+        regroup_q("im", 1)
+        quantise_q("im", 1)
+        regroup_q("re", 1)
+        quantise_q("re", 1)
 
         s_banks = {"re": (left_banks, "left"), "im": (right_banks, "right")}
         s_acc = {}

@@ -18,6 +18,8 @@ BANK = 512
 TILES = CHANNELS // P
 POSITION_TILES = POSITIONS // P
 HEAD_TILES = 3
+Q_VECTOR_POSITIONS = (512, 336)
+EARLY_IM = 2
 BLOCK_TILES = (6, 7)
 VECTOR_POSITIONS = {("im", 0): 352, ("im", 1): 352, ("re", 0): 352, ("re", 1): 352}
 
@@ -106,10 +108,10 @@ def tile_autoregressivelsa_pa_kernel(tc, E_re, E_im, WKQ_re, WKQ_im, out_0, out_
         load_e("im", 0)
         load_w(0)
         load_w(1)
-        load_e("im", 1)
         load_w(2)
-        load_e("re", 0)
+        load_e("im", 1)
         load_w(3)
+        load_e("re", 0)
         load_e("re", 1)
         load_w(4)
         load_w(5)
@@ -218,18 +220,25 @@ def tile_autoregressivelsa_pa_kernel(tc, E_re, E_im, WKQ_re, WKQ_im, out_0, out_
             product(m, "im", g, 1)
             product(m, "re", g, 0)
 
+        def half_tile(m, part):
+            for g in range(PASSES):
+                for xi in range(2):
+                    product(m, part, g, xi)
+            out_q(m, part)
+
         def whole_tile(m):
             for part in ("im", "re"):
-                for g in range(PASSES):
-                    for xi in range(2):
-                        product(m, part, g, xi)
-                out_q(m, part)
+                half_tile(m, part)
 
         q_grouped = {}
 
         def regroup_q(part, g):
             q_grouped[(part, g)] = keep.tile([P, PACK * POSITIONS], BF16, name="q_grp_%s%d" % (part, g), align_bytes=64)
-            regroup(nc.vector.tensor_copy, q_grouped[(part, g)][:], q_raw[part][:, 4 * g : 4 * g + 4, :], 0, POSITIONS)
+            rows = q_raw[part][:, 4 * g : 4 * g + 4, :]
+            cut = Q_VECTOR_POSITIONS[g]
+            regroup(nc.vector.tensor_copy, q_grouped[(part, g)][:], rows, 0, cut)
+            if cut < POSITIONS:
+                regroup(nc.scalar.copy, q_grouped[(part, g)][:], rows, cut, POSITIONS)
 
         def quantise_q(part, g):
             nc.vector.quantize_mx(
@@ -238,35 +247,36 @@ def tile_autoregressivelsa_pa_kernel(tc, E_re, E_im, WKQ_re, WKQ_im, out_0, out_
         regroup_e("im", 0)
         negate_e(0)
         quantise_e("im", 0)
-        transpose_w(0)
-        transpose_w(1)
-        quantise_w(0)
         quantise_e("neg", 0)
-        regroup_e("im", 1)
+        for m in range(3):
+            transpose_w(m)
+        quantise_w(0)
         quantise_w(1)
-        negate_e(1)
-        quantise_e("im", 1)
-        quantise_e("neg", 1)
+        regroup_e("im", 1)
         products_im(0, 0)
-        transpose_w(2)
         products_im(1, 0)
-        regroup_e("re", 0)
-        quantise_e("re", 0)
+        quantise_e("im", 1)
+        negate_e(1)
         transpose_w(3)
-        products_im(0, 1)
-        products_im(1, 1)
+        quantise_e("neg", 1)
+        regroup_e("re", 0)
+        for m in range(2):
+            product(m, "im", 1, 0)
+        for m in range(2):
+            product(m, "re", 1, 1)
+        quantise_e("re", 0)
         regroup_e("re", 1)
-        quantise_e("re", 1)
         transpose_w(4)
-        quantise_w(2)
-        quantise_w(3)
+        transpose_w(5)
         products_re(0, 0)
+        products_re(1, 0)
+        quantise_e("re", 1)
+        quantise_w(2)
         products_re(0, 1)
         out_q(0, "im")
         out_q(0, "re")
-        products_re(1, 0)
         products_re(1, 1)
-        transpose_w(5)
+        quantise_w(3)
         out_q(1, "im")
         out_q(1, "re")
         spread_words(6)
@@ -280,42 +290,64 @@ def tile_autoregressivelsa_pa_kernel(tc, E_re, E_im, WKQ_re, WKQ_im, out_0, out_
         turn_blocks(7)
         whole_tile(3)
         regroup_q("im", 0)
-        regroup_q("re", 0)
-        whole_tile(4)
+        half_tile(4, "im")
         join_words(7)
-        quantise_q("im", 0)
         quantise_w(7)
+        half_tile(4, "re")
+        regroup_q("re", 0)
+        quantise_q("im", 0)
         quantise_q("re", 0)
         for m in range(5, TILES):
-            whole_tile(m)
-        regroup_q("im", 1)
-        quantise_q("im", 1)
-        regroup_q("re", 1)
-        quantise_q("re", 1)
+            for part in ("im", "re"):
+                half_tile(m, part)
+                if m == TILES - 1:
+                    regroup_q(part, 1)
+                    quantise_q(part, 1)
 
         s_banks = {"re": (left_banks, "left"), "im": (right_banks, "right")}
         s_acc = {}
-        for g in range(PASSES):
-            for part in ("re", "im"):
-                for i in range(POSITION_TILES):
-                    if g == 0:
-                        pool, tag = s_banks[part]
-                        s_acc[(part, i)] = pool.tile([P, BANK], F32, name="s_acc", tag=tag)
-                    rows = slice(i * P, (i + 1) * P)
-                    for n, (operand, q_part) in enumerate(STAGE2_TERMS[part]):
-                        nc.tensor.matmul_mx(
-                            out=s_acc[(part, i)][:],
-                            lhsT=e_codes[operand][:, g, rows].bitcast(FP8X4),
-                            lhsT_scale=e_scales[operand][:, g, rows],
-                            rhs=q_codes[q_part][:, g, :].bitcast(FP8X4),
-                            rhs_scale=q_scales[q_part][:, g, :],
-                            start=(g == 0 and n == 0),
-                            stop=(g == PASSES - 1 and n == 1),
-                        )
-                    if g == PASSES - 1:
-                        s_sb = keep.tile([P, POSITIONS], F32, name="s_sb_%s%d" % (part, i))
-                        if i % 2 == 0:
-                            nc.scalar.copy(out=s_sb[:], in_=s_acc[(part, i)][:])
-                        else:
-                            nc.vector.tensor_copy(out=s_sb[:], in_=s_acc[(part, i)][:])
-                        nc.sync.dma_start(out=s_dram[part][0, rows, :], in_=s_sb[:])
+
+        def s_products(part, i, g, columns):
+            key = (part, i, columns.start)
+            if key not in s_acc:
+                pool, tag = s_banks[part]
+                s_acc[key] = pool.tile([P, BANK], F32, name="s_acc", tag=tag)
+            rows = slice(i * P, (i + 1) * P)
+            width = columns.stop - columns.start
+            for n, (operand, q_part) in enumerate(STAGE2_TERMS[part]):
+                nc.tensor.matmul_mx(
+                    out=s_acc[key][:, 0:width],
+                    lhsT=e_codes[operand][:, g, rows].bitcast(FP8X4),
+                    lhsT_scale=e_scales[operand][:, g, rows],
+                    rhs=q_codes[q_part][:, g, columns].bitcast(FP8X4),
+                    rhs_scale=q_scales[q_part][:, g, columns],
+                    start=(g == 0 and n == 0),
+                    stop=(g == PASSES - 1 and n == 1),
+                )
+
+        def store_s(part, i, columns, copy):
+            width = columns.stop - columns.start
+            s_sb = keep.tile([P, width], F32, name="s_sb_%s%d_%d" % (part, i, columns.start))
+            copy(out=s_sb[:], in_=s_acc[(part, i, columns.start)][:, 0:width])
+            nc.sync.dma_start(out=s_dram[part][0, i * P : (i + 1) * P, columns], in_=s_sb[:])
+
+        whole = slice(0, POSITIONS)
+        early = [("re", i) for i in range(POSITION_TILES)] + [("im", i) for i in range(EARLY_IM)]
+        late = [("im", i) for i in range(EARLY_IM, POSITION_TILES)]
+        for part, i in early:
+            s_products(part, i, 0, whole)
+        copies = (nc.scalar.copy, nc.vector.tensor_copy)
+        stored = 0
+        for part, i in early:
+            s_products(part, i, 1, whole)
+            store_s(part, i, whole, copies[stored % 2])
+            stored += 1
+        for part, i in late:
+            pieces = [whole]
+            if (part, i) == late[-1]:
+                pieces = [slice(0, POSITIONS // 2), slice(POSITIONS // 2, POSITIONS)]
+            for columns in pieces:
+                for g in range(PASSES):
+                    s_products(part, i, g, columns)
+                store_s(part, i, columns, copies[stored % 2])
+                stored += 1

@@ -48,6 +48,14 @@ def tile_autoregressivelsa_pa_kernel(tc, E_re, E_im, WKQ_re, WKQ_im, out_0, out_
         right_banks = ctx.enter_context(tc.psum_pool(name="right_banks", bufs=4))
         ctx.enter_context(tc.manual_schedule())
 
+        zeros = keep.tile([P, BANK], BF16, name="zeros")
+        nc.vector.memset(zeros[:], 0.0)
+
+        def keep_warm(count):
+            for i in range(count):
+                bank = left_banks.tile([P, BANK], F32, name="idle_bank", tag="left")
+                nc.tensor.matmul(bank[:], lhsT=zeros[:, 0:P], rhs=zeros[:], start=True, stop=True)
+
         identity = keep.tile([P, P], F32, name="identity")
         make_identity(nc, identity[:])
 
@@ -108,10 +116,10 @@ def tile_autoregressivelsa_pa_kernel(tc, E_re, E_im, WKQ_re, WKQ_im, out_0, out_
         load_e("im", 0)
         load_w(0)
         load_w(1)
-        load_w(2)
         load_e("im", 1)
-        load_w(3)
+        load_w(2)
         load_e("re", 0)
+        load_w(3)
         load_e("re", 1)
         load_w(4)
         load_w(5)
@@ -248,35 +256,37 @@ def tile_autoregressivelsa_pa_kernel(tc, E_re, E_im, WKQ_re, WKQ_im, out_0, out_
         negate_e(0)
         quantise_e("im", 0)
         quantise_e("neg", 0)
-        for m in range(3):
-            transpose_w(m)
+        keep_warm(6)
+        transpose_w(0)
+        keep_warm(2)
+        transpose_w(1)
+        keep_warm(2)
         quantise_w(0)
-        quantise_w(1)
         regroup_e("im", 1)
-        products_im(0, 0)
-        products_im(1, 0)
-        quantise_e("im", 1)
+        quantise_w(1)
         negate_e(1)
-        transpose_w(3)
+        quantise_e("im", 1)
         quantise_e("neg", 1)
+        products_im(0, 0)
+        transpose_w(2)
+        products_im(1, 0)
         regroup_e("re", 0)
-        for m in range(2):
-            product(m, "im", 1, 0)
-        for m in range(2):
-            product(m, "re", 1, 1)
         quantise_e("re", 0)
+        transpose_w(3)
+        products_im(0, 1)
+        products_im(1, 1)
         regroup_e("re", 1)
-        transpose_w(4)
-        transpose_w(5)
-        products_re(0, 0)
-        products_re(1, 0)
         quantise_e("re", 1)
+        transpose_w(4)
         quantise_w(2)
+        quantise_w(3)
+        products_re(0, 0)
         products_re(0, 1)
         out_q(0, "im")
         out_q(0, "re")
+        products_re(1, 0)
         products_re(1, 1)
-        quantise_w(3)
+        transpose_w(5)
         out_q(1, "im")
         out_q(1, "re")
         spread_words(6)

@@ -18,15 +18,15 @@ BANK = 512
 TILES = CHANNELS // P
 POSITION_TILES = POSITIONS // P
 HEAD_TILES = 3
-Q_VECTOR_POSITIONS = (512, 336)
+Q_VECTOR_POSITIONS = (352, 336)
 EARLY_IM = 2
-BLOCK_TILES = (6, 7)
+BLOCK_TILES = (5, 6, 7)
 VECTOR_POSITIONS = {("im", 0): 352, ("im", 1): 352, ("re", 0): 352, ("re", 1): 352}
 
 FLOPS = 2 * 4 * CHANNELS * CHANNELS * POSITIONS + 2 * 4 * POSITIONS * CHANNELS * POSITIONS
 
 STAGE1_E = {"re": ("re", "neg"), "im": ("im", "re")}
-STAGE2_TERMS = {"re": (("re", "re"), ("im", "im")), "im": (("re", "im"), ("neg", "re"))}
+STAGE2_TERMS = {"re": (("im", "im"), ("re", "re")), "im": (("re", "im"), ("neg", "re"))}
 
 
 def regroup(engine_copy, grouped, rows, first, last):
@@ -47,14 +47,6 @@ def tile_autoregressivelsa_pa_kernel(tc, E_re, E_im, WKQ_re, WKQ_im, out_0, out_
         left_banks = ctx.enter_context(tc.psum_pool(name="left_banks", bufs=4))
         right_banks = ctx.enter_context(tc.psum_pool(name="right_banks", bufs=4))
         ctx.enter_context(tc.manual_schedule())
-
-        zeros = keep.tile([P, BANK], BF16, name="zeros")
-        nc.vector.memset(zeros[:], 0.0)
-
-        def keep_warm(count):
-            for i in range(count):
-                bank = left_banks.tile([P, BANK], F32, name="idle_bank", tag="left")
-                nc.tensor.matmul(bank[:], lhsT=zeros[:, 0:P], rhs=zeros[:], start=True, stop=True)
 
         identity = keep.tile([P, P], F32, name="identity")
         make_identity(nc, identity[:])
@@ -122,7 +114,6 @@ def tile_autoregressivelsa_pa_kernel(tc, E_re, E_im, WKQ_re, WKQ_im, out_0, out_
         load_w(3)
         load_e("re", 1)
         load_w(4)
-        load_w(5)
         for m in BLOCK_TILES:
             load_w_blocks(m)
 
@@ -171,24 +162,33 @@ def tile_autoregressivelsa_pa_kernel(tc, E_re, E_im, WKQ_re, WKQ_im, out_0, out_
                     in_=bank[:].rearrange("p (g u m) -> p g m u", g=PASSES, u=2, m=P),
                 )
 
-        def spread_words(m):
-            w_perm[m] = keep.tile([P, 2 * BANK], F32, name="w_perm%d" % m, align_bytes=64)
+        def spread_words(m, xi):
+            w_perm[(m, xi)] = keep.tile([P, BANK], F32, name="w_perm%d%d" % (m, xi), align_bytes=64)
             nc.vector.tensor_copy(
-                out=w_perm[m][:].rearrange("p (s u c) -> p s u c", u=2, c=32),
-                in_=w_raw[m][:].rearrange("p x g n k -> p (x g n k)").bitcast(F32).rearrange(
+                out=w_perm[(m, xi)][:].rearrange("p (s u c) -> p s u c", u=2, c=32),
+                in_=w_raw[m][:, xi, :, :, :].rearrange("p g n k -> p (g n k)").bitcast(F32).rearrange(
                     "p (s c u) -> p s u c", c=32, u=2
                 ),
             )
 
-        def turn_blocks(m):
-            w_turned[m] = keep.tile([P, 2 * BANK], F32, name="w_turned%d" % m, align_bytes=64)
-            nc.vector.transpose(out=w_turned[m][:], in_=w_perm[m][:])
+        def turn_blocks(m, xi):
+            w_turned[(m, xi)] = keep.tile([P, BANK], F32, name="w_turned%d%d" % (m, xi), align_bytes=64)
+            nc.vector.transpose(out=w_turned[(m, xi)][:], in_=w_perm[(m, xi)][:])
 
-        def join_words(m):
-            w_grouped[m] = keep.tile([P, 2 * BANK], F32, name="w_grp_%d" % m, align_bytes=64)
+        def join_words(m, xi):
+            if xi == 0:
+                w_grouped[m] = keep.tile([P, 2 * BANK], F32, name="w_grp_%d" % m, align_bytes=64)
             nc.scalar.copy(
-                out=w_grouped[m][:].rearrange("p (s r u) -> p s r u", r=32, u=2),
-                in_=w_turned[m][:].rearrange("p (s u r) -> p s r u", u=2, r=32),
+                out=w_grouped[m][:, xi * BANK : (xi + 1) * BANK].rearrange("p (s r u) -> p s r u", r=32, u=2),
+                in_=w_turned[(m, xi)][:].rearrange("p (s u r) -> p s r u", u=2, r=32),
+            )
+
+        def quantise_w_half(m, xi):
+            columns = slice(xi * PASSES * P, (xi + 1) * PASSES * P)
+            nc.vector.quantize_mx(
+                out=w_codes[:, m, columns].bitcast(FP8X4),
+                scales=w_scales[:, m, columns],
+                in_=w_grouped[m][:, xi * BANK : (xi + 1) * BANK].bitcast(BF16),
             )
 
         def quantise_w(m):
@@ -229,8 +229,8 @@ def tile_autoregressivelsa_pa_kernel(tc, E_re, E_im, WKQ_re, WKQ_im, out_0, out_
             product(m, "re", g, 0)
 
         def half_tile(m, part):
-            for g in range(PASSES):
-                for xi in range(2):
+            for xi in range(2):
+                for g in range(PASSES):
                     product(m, part, g, xi)
             out_q(m, part)
 
@@ -256,11 +256,8 @@ def tile_autoregressivelsa_pa_kernel(tc, E_re, E_im, WKQ_re, WKQ_im, out_0, out_
         negate_e(0)
         quantise_e("im", 0)
         quantise_e("neg", 0)
-        keep_warm(6)
         transpose_w(0)
-        keep_warm(2)
         transpose_w(1)
-        keep_warm(2)
         quantise_w(0)
         regroup_e("im", 1)
         quantise_w(1)
@@ -279,35 +276,48 @@ def tile_autoregressivelsa_pa_kernel(tc, E_re, E_im, WKQ_re, WKQ_im, out_0, out_
         quantise_e("re", 1)
         transpose_w(4)
         quantise_w(2)
-        quantise_w(3)
         products_re(0, 0)
+        products_re(1, 0)
         products_re(0, 1)
         out_q(0, "im")
         out_q(0, "re")
-        products_re(1, 0)
         products_re(1, 1)
-        transpose_w(5)
         out_q(1, "im")
         out_q(1, "re")
-        spread_words(6)
-        quantise_w(4)
-        turn_blocks(6)
-        quantise_w(5)
+        spread_words(5, 0)
+        turn_blocks(5, 0)
+        quantise_w(3)
+        spread_words(5, 1)
+        turn_blocks(5, 1)
         whole_tile(2)
-        join_words(6)
-        spread_words(7)
-        quantise_w(6)
-        turn_blocks(7)
+        join_words(5, 0)
+        join_words(5, 1)
+        quantise_w(4)
+        spread_words(6, 0)
+        turn_blocks(6, 0)
+        quantise_w(5)
         whole_tile(3)
+        spread_words(6, 1)
+        turn_blocks(6, 1)
+        join_words(6, 0)
+        join_words(6, 1)
+        spread_words(7, 0)
+        turn_blocks(7, 0)
+        quantise_w(6)
+        whole_tile(4)
+        join_words(7, 0)
+        spread_words(7, 1)
+        turn_blocks(7, 1)
         regroup_q("im", 0)
-        half_tile(4, "im")
-        join_words(7)
-        quantise_w(7)
-        half_tile(4, "re")
+        half_tile(5, "im")
+        join_words(7, 1)
+        quantise_w_half(7, 0)
+        quantise_w_half(7, 1)
         regroup_q("re", 0)
         quantise_q("im", 0)
         quantise_q("re", 0)
-        for m in range(5, TILES):
+        half_tile(5, "re")
+        for m in range(6, TILES):
             for part in ("im", "re"):
                 half_tile(m, part)
                 if m == TILES - 1:
@@ -317,23 +327,22 @@ def tile_autoregressivelsa_pa_kernel(tc, E_re, E_im, WKQ_re, WKQ_im, out_0, out_
         s_banks = {"re": (left_banks, "left"), "im": (right_banks, "right")}
         s_acc = {}
 
-        def s_products(part, i, g, columns):
+        def s_product(part, i, g, n, columns):
             key = (part, i, columns.start)
             if key not in s_acc:
                 pool, tag = s_banks[part]
                 s_acc[key] = pool.tile([P, BANK], F32, name="s_acc", tag=tag)
             rows = slice(i * P, (i + 1) * P)
-            width = columns.stop - columns.start
-            for n, (operand, q_part) in enumerate(STAGE2_TERMS[part]):
-                nc.tensor.matmul_mx(
-                    out=s_acc[key][:, 0:width],
-                    lhsT=e_codes[operand][:, g, rows].bitcast(FP8X4),
-                    lhsT_scale=e_scales[operand][:, g, rows],
-                    rhs=q_codes[q_part][:, g, columns].bitcast(FP8X4),
-                    rhs_scale=q_scales[q_part][:, g, columns],
-                    start=(g == 0 and n == 0),
-                    stop=(g == PASSES - 1 and n == 1),
-                )
+            operand, q_part = STAGE2_TERMS[part][n]
+            nc.tensor.matmul_mx(
+                out=s_acc[key][:, 0 : columns.stop - columns.start],
+                lhsT=e_codes[operand][:, g, rows].bitcast(FP8X4),
+                lhsT_scale=e_scales[operand][:, g, rows],
+                rhs=q_codes[q_part][:, g, columns].bitcast(FP8X4),
+                rhs_scale=q_scales[q_part][:, g, columns],
+                start=(g == 0 and n == 0),
+                stop=(g == PASSES - 1 and n == 1),
+            )
 
         def store_s(part, i, columns, copy):
             width = columns.stop - columns.start
@@ -345,19 +354,24 @@ def tile_autoregressivelsa_pa_kernel(tc, E_re, E_im, WKQ_re, WKQ_im, out_0, out_
         early = [("re", i) for i in range(POSITION_TILES)] + [("im", i) for i in range(EARLY_IM)]
         late = [("im", i) for i in range(EARLY_IM, POSITION_TILES)]
         for part, i in early:
-            s_products(part, i, 0, whole)
+            for n in range(2):
+                s_product(part, i, 0, n, whole)
         copies = (nc.scalar.copy, nc.vector.tensor_copy)
         stored = 0
-        for part, i in early:
-            s_products(part, i, 1, whole)
-            store_s(part, i, whole, copies[stored % 2])
-            stored += 1
+        for pair in range(0, len(early), 2):
+            for n in range(2):
+                for part, i in early[pair : pair + 2]:
+                    s_product(part, i, 1, n, whole)
+                    if n == 1:
+                        store_s(part, i, whole, copies[stored % 2])
+                        stored += 1
         for part, i in late:
             pieces = [whole]
             if (part, i) == late[-1]:
                 pieces = [slice(0, POSITIONS // 2), slice(POSITIONS // 2, POSITIONS)]
             for columns in pieces:
                 for g in range(PASSES):
-                    s_products(part, i, g, columns)
+                    for n in range(2):
+                        s_product(part, i, g, n, columns)
                 store_s(part, i, columns, copies[stored % 2])
                 stored += 1

@@ -20,7 +20,7 @@ POSITION_TILES = POSITIONS // P
 HEAD_TILES = 3
 Q_VECTOR_POSITIONS = (352, 336)
 EARLY_IM = 2
-BLOCK_TILES = (5, 6, 7)
+BLOCK_TILES = (6, 7)
 VECTOR_POSITIONS = {("im", 0): 352, ("im", 1): 352, ("re", 0): 352, ("re", 1): 352}
 
 FLOPS = 2 * 4 * CHANNELS * CHANNELS * POSITIONS + 2 * 4 * POSITIONS * CHANNELS * POSITIONS
@@ -114,6 +114,7 @@ def tile_autoregressivelsa_pa_kernel(tc, E_re, E_im, WKQ_re, WKQ_im, out_0, out_
         load_w(3)
         load_e("re", 1)
         load_w(4)
+        load_w(5)
         for m in BLOCK_TILES:
             load_w_blocks(m)
 
@@ -276,27 +277,22 @@ def tile_autoregressivelsa_pa_kernel(tc, E_re, E_im, WKQ_re, WKQ_im, out_0, out_
         quantise_e("re", 1)
         transpose_w(4)
         quantise_w(2)
+        permute_w(5)
         products_re(0, 0)
         products_re(1, 0)
         products_re(0, 1)
         out_q(0, "im")
         out_q(0, "re")
         products_re(1, 1)
+        transpose_w(5)
         out_q(1, "im")
         out_q(1, "re")
-        spread_words(5, 0)
-        turn_blocks(5, 0)
         quantise_w(3)
-        spread_words(5, 1)
-        turn_blocks(5, 1)
-        whole_tile(2)
-        join_words(5, 0)
-        join_words(5, 1)
         quantise_w(4)
         spread_words(6, 0)
         turn_blocks(6, 0)
         quantise_w(5)
-        whole_tile(3)
+        whole_tile(2)
         spread_words(6, 1)
         turn_blocks(6, 1)
         join_words(6, 0)
@@ -304,18 +300,19 @@ def tile_autoregressivelsa_pa_kernel(tc, E_re, E_im, WKQ_re, WKQ_im, out_0, out_
         spread_words(7, 0)
         turn_blocks(7, 0)
         quantise_w(6)
-        whole_tile(4)
-        join_words(7, 0)
+        whole_tile(3)
         spread_words(7, 1)
         turn_blocks(7, 1)
         regroup_q("im", 0)
-        half_tile(5, "im")
+        half_tile(4, "im")
+        join_words(7, 0)
         join_words(7, 1)
-        quantise_w_half(7, 0)
-        quantise_w_half(7, 1)
+        quantise_w(7)
+        half_tile(4, "re")
         regroup_q("re", 0)
         quantise_q("im", 0)
         quantise_q("re", 0)
+        half_tile(5, "im")
         half_tile(5, "re")
         for m in range(6, TILES):
             for part in ("im", "re"):

from contextlib import ExitStack

import concourse.mybir as mybir
from concourse.masks import make_identity

BF16 = mybir.dt.bfloat16
F32 = mybir.dt.float32
U32 = mybir.dt.uint32
U8 = mybir.dt.uint8
FP8X4 = mybir.dt.float8_e4m3fn_x4

P = 128
PACK = 4
CHANNELS = 1024
POSITIONS = 512
PASSES = CHANNELS // (P * PACK)
BANK = 512
TILES = CHANNELS // P
POSITION_TILES = POSITIONS // P
HEAD_TILES = 3
Q_VECTOR_POSITIONS = (352, 336)
EARLY_IM = 2
BLOCK_TILES = (6, 7)
VECTOR_POSITIONS = {("im", 0): 352, ("im", 1): 352, ("re", 0): 352, ("re", 1): 352}

FLOPS = 2 * 4 * CHANNELS * CHANNELS * POSITIONS + 2 * 4 * POSITIONS * CHANNELS * POSITIONS

STAGE1_E = {"re": ("re", "neg"), "im": ("im", "re")}
STAGE2_TERMS = {"re": (("im", "im"), ("re", "re")), "im": (("re", "im"), ("neg", "re"))}


def regroup(engine_copy, grouped, rows, first, last):
    engine_copy(
        out=grouped.rearrange("p (c i j) -> p c j i", i=4, j=PACK)[:, first // 4 : last // 4, :, :],
        in_=rows.rearrange("p j (c i) -> p c j i", i=4)[:, first // 4 : last // 4, :, :],
    )


def tile_autoregressivelsa_pa_kernel(tc, E_re, E_im, WKQ_re, WKQ_im, out_0, out_1):
    nc = tc.nc
    e_dram = {"re": E_re, "im": E_im}
    w_dram = {"re": WKQ_re, "im": WKQ_im}
    s_dram = {"re": out_0, "im": out_1}

    with ExitStack() as ctx:
        keep = ctx.enter_context(tc.tile_pool(name="keep", bufs=1))
        left_banks = ctx.enter_context(tc.psum_pool(name="left_banks", bufs=4))
        right_banks = ctx.enter_context(tc.psum_pool(name="right_banks", bufs=4))
        ctx.enter_context(tc.manual_schedule())

        identity = keep.tile([P, P], F32, name="identity")
        make_identity(nc, identity[:])

        e_raw = {}
        e_grouped = {}
        for x in ("re", "im", "neg"):
            for g in range(PASSES):
                if x != "neg":
                    e_raw[(x, g)] = keep.tile([P, PACK, POSITIONS], BF16, name="e_raw_%s%d" % (x, g))
                e_grouped[(x, g)] = keep.tile(
                    [P, PACK * POSITIONS], BF16, name="e_grp_%s%d" % (x, g), align_bytes=64
                )
        e_codes = {}
        e_scales = {}
        for x in ("re", "im", "neg"):
            e_codes[x] = keep.tile([P, PASSES, POSITIONS], U32, name="e_codes_" + x, align_bytes=64)
            e_scales[x] = keep.tile([P, PASSES, POSITIONS], U8, name="e_scales_" + x, align_bytes=64)
        w_raw = {}
        for m in range(TILES):
            if m in BLOCK_TILES:
                w_raw[m] = keep.tile([P, 2, PASSES, 4, P], BF16, name="w_raw%d" % m)
            else:
                w_raw[m] = keep.tile([P, 2, CHANNELS], BF16, name="w_raw%d" % m)
        w_codes = keep.tile([P, TILES, 2 * PASSES * P], U32, name="w_codes", align_bytes=64)
        w_scales = keep.tile([P, TILES, 2 * PASSES * P], U8, name="w_scales", align_bytes=64)
        q_raw = {}
        q_codes = {}
        q_scales = {}
        for part in ("re", "im"):
            q_raw[part] = keep.tile([P, TILES, POSITIONS], BF16, name="q_raw_" + part)
            q_codes[part] = keep.tile([P, PASSES, POSITIONS], U32, name="q_codes_" + part, align_bytes=64)
            q_scales[part] = keep.tile([P, PASSES, POSITIONS], U8, name="q_scales_" + part, align_bytes=64)

        def load_e(x, g):
            nc.sync.dma_start(
                out=e_raw[(x, g)][:].rearrange("p j t -> p (j t)"),
                in_=e_dram[x].rearrange("b (g p j) t -> b g p (j t)", g=PASSES, p=P, j=PACK)[0, g, :, :],
            )

        def load_w_blocks(m):
            for xi, x in enumerate(("re", "im")):
                for g in range(PASSES):
                    for a in range(4):
                        nc.sync.dma_start(
                            out=w_raw[m][32 * a : 32 * a + 32, xi, g, :, :],
                            in_=w_dram[x].rearrange("(h n r t) (g a k) -> h t g a r n k", n=4, r=32, t=PACK, g=PASSES, a=4)[
                                m // 4, m % 4, g, a, :, :, :
                            ],
                        )

        def load_w(m):
            for xi, x in enumerate(("re", "im")):
                nc.sync.dma_start(
                    out=w_raw[m][:, xi, :],
                    in_=w_dram[x].rearrange("(g p j) c -> g j p c", g=PASSES, p=P, j=PACK)[m // 4, m % 4, :, :],
                )

        load_e("im", 0)
        load_w(0)
        load_w(1)
        load_e("im", 1)
        load_w(2)
        load_e("re", 0)
        load_w(3)
        load_e("re", 1)
        load_w(4)
        load_w(5)
        for m in BLOCK_TILES:
            load_w_blocks(m)

        def regroup_e(x, g):
            cut = VECTOR_POSITIONS[(x, g)]
            regroup(nc.vector.tensor_copy, e_grouped[(x, g)][:], e_raw[(x, g)][:], 0, cut)
            regroup(nc.scalar.copy, e_grouped[(x, g)][:], e_raw[(x, g)][:], cut, POSITIONS)

        def negate_e(g):
            nc.vector.tensor_scalar_mul(out=e_grouped[("neg", g)][:], in0=e_grouped[("im", g)][:], scalar1=-1.0)

        def quantise_e(x, g):
            nc.vector.quantize_mx(
                out=e_codes[x][:, g, :].bitcast(FP8X4), scales=e_scales[x][:, g, :], in_=e_grouped[(x, g)][:]
            )

        w_grouped = {}
        w_perm = {}
        w_turned = {}

        def permute_w(m):
            w_perm[m] = keep.tile([P, 2 * PASSES, 2, P], F32, name="w_perm%d" % m)
            nc.vector.tensor_copy(
                out=w_perm[m][:],
                in_=w_raw[m][:].rearrange("p x c -> p (x c)").bitcast(F32).rearrange(
                    "p (g c u) -> p g u c", g=2 * PASSES, c=P, u=2
                ),
            )

        def transpose_w(m):
            w_grouped[m] = keep.tile([P, 2 * BANK], F32, name="w_grp_%d" % m, align_bytes=64)
            for xi in range(2):
                words_in = w_raw[m][:, xi, :].bitcast(F32)
                bank = left_banks.tile([P, BANK], F32, name="w_bank", tag="left")
                for g in range(PASSES):
                    for u in range(2):
                        if m in w_perm:
                            in_ = w_perm[m][:, PASSES * xi + g, u, :]
                        else:
                            in_ = words_in[:, 2 * P * g + u : 2 * P * (g + 1) : 2]
                        nc.tensor.transpose(bank[:, (2 * g + u) * P : (2 * g + u + 1) * P], in_, identity[:])
                nc.scalar.copy(
                    out=w_grouped[m][:, xi * BANK : (xi + 1) * BANK].rearrange(
                        "p (g m u) -> p g m u", g=PASSES, m=P, u=2
                    ),
                    in_=bank[:].rearrange("p (g u m) -> p g m u", g=PASSES, u=2, m=P),
                )

        def spread_words(m, xi):
            w_perm[(m, xi)] = keep.tile([P, BANK], F32, name="w_perm%d%d" % (m, xi), align_bytes=64)
            nc.vector.tensor_copy(
                out=w_perm[(m, xi)][:].rearrange("p (s u c) -> p s u c", u=2, c=32),
                in_=w_raw[m][:, xi, :, :, :].rearrange("p g n k -> p (g n k)").bitcast(F32).rearrange(
                    "p (s c u) -> p s u c", c=32, u=2
                ),
            )

        def turn_blocks(m, xi):
            w_turned[(m, xi)] = keep.tile([P, BANK], F32, name="w_turned%d%d" % (m, xi), align_bytes=64)
            nc.vector.transpose(out=w_turned[(m, xi)][:], in_=w_perm[(m, xi)][:])

        def join_words(m, xi):
            if xi == 0:
                w_grouped[m] = keep.tile([P, 2 * BANK], F32, name="w_grp_%d" % m, align_bytes=64)
            nc.scalar.copy(
                out=w_grouped[m][:, xi * BANK : (xi + 1) * BANK].rearrange("p (s r u) -> p s r u", r=32, u=2),
                in_=w_turned[(m, xi)][:].rearrange("p (s u r) -> p s r u", u=2, r=32),
            )

        def quantise_w_half(m, xi):
            columns = slice(xi * PASSES * P, (xi + 1) * PASSES * P)
            nc.vector.quantize_mx(
                out=w_codes[:, m, columns].bitcast(FP8X4),
                scales=w_scales[:, m, columns],
                in_=w_grouped[m][:, xi * BANK : (xi + 1) * BANK].bitcast(BF16),
            )

        def quantise_w(m):
            nc.vector.quantize_mx(
                out=w_codes[:, m, :].bitcast(FP8X4), scales=w_scales[:, m, :], in_=w_grouped[m][:].bitcast(BF16)
            )

        q_acc = {}
        q_done = {}

        def product(m, part, g, xi):
            if (m, part) not in q_acc:
                q_acc[(m, part)] = right_banks.tile([P, BANK], F32, name="q_acc", tag="right")
                q_done[(m, part)] = 0
            acc = q_acc[(m, part)]
            operand = STAGE1_E[part][xi]
            w_cols = slice((xi * PASSES + g) * P, (xi * PASSES + g + 1) * P)
            nc.tensor.matmul_mx(
                out=acc[:],
                lhsT=w_codes[:, m, w_cols].bitcast(FP8X4),
                lhsT_scale=w_scales[:, m, w_cols],
                rhs=e_codes[operand][:, g, :].bitcast(FP8X4),
                rhs_scale=e_scales[operand][:, g, :],
                start=q_done[(m, part)] == 0,
                stop=q_done[(m, part)] == 3,
            )
            q_done[(m, part)] += 1

        def out_q(m, part):
            nc.scalar.copy(out=q_raw[part][:, m, :], in_=q_acc[(m, part)][:])

        def products_im(m, g):
            product(m, "im", g, 0)
            product(m, "re", g, 1)

        def products_re(m, g):
            product(m, "im", g, 1)
            product(m, "re", g, 0)

        def half_tile(m, part):
            for xi in range(2):
                for g in range(PASSES):
                    product(m, part, g, xi)
            out_q(m, part)

        def whole_tile(m):
            for part in ("im", "re"):
                half_tile(m, part)

        q_grouped = {}

        def regroup_q(part, g):
            q_grouped[(part, g)] = keep.tile([P, PACK * POSITIONS], BF16, name="q_grp_%s%d" % (part, g), align_bytes=64)
            rows = q_raw[part][:, 4 * g : 4 * g + 4, :]
            cut = Q_VECTOR_POSITIONS[g]
            regroup(nc.vector.tensor_copy, q_grouped[(part, g)][:], rows, 0, cut)
            if cut < POSITIONS:
                regroup(nc.scalar.copy, q_grouped[(part, g)][:], rows, cut, POSITIONS)

        def quantise_q(part, g):
            nc.vector.quantize_mx(
                out=q_codes[part][:, g, :].bitcast(FP8X4), scales=q_scales[part][:, g, :], in_=q_grouped[(part, g)][:]
            )
        regroup_e("im", 0)
        negate_e(0)
        quantise_e("im", 0)
        quantise_e("neg", 0)
        transpose_w(0)
        transpose_w(1)
        quantise_w(0)
        regroup_e("im", 1)
        quantise_w(1)
        negate_e(1)
        quantise_e("im", 1)
        quantise_e("neg", 1)
        products_im(0, 0)
        transpose_w(2)
        products_im(1, 0)
        regroup_e("re", 0)
        quantise_e("re", 0)
        transpose_w(3)
        products_im(0, 1)
        products_im(1, 1)
        regroup_e("re", 1)
        quantise_e("re", 1)
        transpose_w(4)
        quantise_w(2)
        permute_w(5)
        products_re(0, 0)
        products_re(1, 0)
        products_re(0, 1)
        out_q(0, "im")
        out_q(0, "re")
        products_re(1, 1)
        transpose_w(5)
        out_q(1, "im")
        out_q(1, "re")
        quantise_w(3)
        quantise_w(4)
        spread_words(6, 0)
        turn_blocks(6, 0)
        quantise_w(5)
        whole_tile(2)
        spread_words(6, 1)
        turn_blocks(6, 1)
        join_words(6, 0)
        join_words(6, 1)
        spread_words(7, 0)
        turn_blocks(7, 0)
        quantise_w(6)
        whole_tile(3)
        spread_words(7, 1)
        turn_blocks(7, 1)
        regroup_q("im", 0)
        half_tile(4, "im")
        join_words(7, 0)
        join_words(7, 1)
        quantise_w(7)
        half_tile(4, "re")
        regroup_q("re", 0)
        quantise_q("im", 0)
        quantise_q("re", 0)
        half_tile(5, "im")
        half_tile(5, "re")
        for m in range(6, TILES):
            for part in ("im", "re"):
                half_tile(m, part)
                if m == TILES - 1:
                    regroup_q(part, 1)
                    quantise_q(part, 1)

        s_banks = {"re": (left_banks, "left"), "im": (right_banks, "right")}
        s_acc = {}

        def s_product(part, i, g, n, columns):
            key = (part, i, columns.start)
            if key not in s_acc:
                pool, tag = s_banks[part]
                s_acc[key] = pool.tile([P, BANK], F32, name="s_acc", tag=tag)
            rows = slice(i * P, (i + 1) * P)
            operand, q_part = STAGE2_TERMS[part][n]
            nc.tensor.matmul_mx(
                out=s_acc[key][:, 0 : columns.stop - columns.start],
                lhsT=e_codes[operand][:, g, rows].bitcast(FP8X4),
                lhsT_scale=e_scales[operand][:, g, rows],
                rhs=q_codes[q_part][:, g, columns].bitcast(FP8X4),
                rhs_scale=q_scales[q_part][:, g, columns],
                start=(g == 0 and n == 0),
                stop=(g == PASSES - 1 and n == 1),
            )

        def store_s(part, i, columns, copy):
            width = columns.stop - columns.start
            s_sb = keep.tile([P, width], F32, name="s_sb_%s%d_%d" % (part, i, columns.start))
            copy(out=s_sb[:], in_=s_acc[(part, i, columns.start)][:, 0:width])
            nc.sync.dma_start(out=s_dram[part][0, i * P : (i + 1) * P, columns], in_=s_sb[:])

        whole = slice(0, POSITIONS)
        early = [("re", i) for i in range(POSITION_TILES)] + [("im", i) for i in range(EARLY_IM)]
        late = [("im", i) for i in range(EARLY_IM, POSITION_TILES)]
        for part, i in early:
            for n in range(2):
                s_product(part, i, 0, n, whole)
        copies = (nc.scalar.copy, nc.vector.tensor_copy)
        stored = 0
        for pair in range(0, len(early), 2):
            for n in range(2):
                for part, i in early[pair : pair + 2]:
                    s_product(part, i, 1, n, whole)
                    if n == 1:
                        store_s(part, i, whole, copies[stored % 2])
                        stored += 1
        for part, i in late:
            pieces = [whole]
            if (part, i) == late[-1]:
                pieces = [slice(0, POSITIONS // 2), slice(POSITIONS // 2, POSITIONS)]
            for columns in pieces:
                for g in range(PASSES):
                    for n in range(2):
                        s_product(part, i, g, n, columns)
                store_s(part, i, columns, copies[stored % 2])
                stored += 1
